import numpy as np
import ml_dtypes


def mxq(x, axis, fmt="e4m3"):
    dtype, down = {"e4m3": (ml_dtypes.float8_e4m3fn, 7), "e5m2": (ml_dtypes.float8_e5m2, 14)}[fmt]
    v = np.moveaxis(np.asarray(x, np.float32).astype(ml_dtypes.bfloat16).astype(np.float64), axis, -1)
    blocks = v.reshape(v.shape[:-1] + (-1, 32))
    amax = np.abs(blocks).max(-1, keepdims=True)
    byte = np.maximum(np.where(amax > 0, np.frexp(amax)[1] - 1 + 127, 0) - down, 1)
    scale = np.exp2(byte - 127.0)
    codes = (blocks / scale).astype(np.float32).astype(dtype).astype(np.float64)
    return np.moveaxis((codes * scale).reshape(v.shape), -1, axis)


WIDE = False


def mx_kscale(k):
    if not WIDE:
        return np.ones(k)
    levels = np.array([10, -10, 5, -5, 0])
    a = np.random.permutation(np.resize(levels, k // 512 * 4)).reshape(k // 512, 4)
    idx = np.arange(k)
    return np.exp2(a[idx // 512, idx % 128 // 32])


BF16 = ml_dtypes.bfloat16


def bf(x):
    return np.asarray(x, np.float32).astype(BF16)


def f64(x):
    return np.asarray(x).astype(np.float64)


E2M1 = np.array([0.0, 0.5, 1.0, 1.5, 2.0, 3.0, 4.0, 6.0, -0.0, -0.5, -1.0, -1.5, -2.0, -3.0, -4.0, -6.0])


def pack_weight(w, fmt):
    k, n = w.shape
    w = f64(bf(w)).reshape(k // 32, 32, n)
    amax = np.abs(w).max(1)
    if fmt == "e4m3":
        byte = np.frexp(amax)[1] - 1 + 127 - 7
    else:
        mant, ex = np.frexp(amax / 6.0)
        byte = np.where(mant > 0.5, ex, ex - 1) + 127
    byte = np.clip(np.where(amax > 0, byte, 1), 1, 254)
    scaled = (w * np.exp2(127.0 - byte)[:, None, :]).reshape(k, n).astype(np.float32)
    by_word = np.ascontiguousarray(scaled.reshape(k // 512, 128, 4, n).transpose(0, 1, 3, 2))
    if fmt == "e4m3":
        words = by_word.astype(ml_dtypes.float8_e4m3fn).view(np.uint8)
    else:
        c = by_word.astype(ml_dtypes.float4_e2m1fn).view(np.uint8) & 0xF
        words = c[..., 0::2] | (c[..., 1::2] << 4)
    return np.ascontiguousarray(words), np.ascontiguousarray(byte.astype(np.uint8).reshape(k // 512, 16, n))


def unpack_weight(words, scales, fmt):
    g, p, n, _ = words.shape
    if fmt == "e4m3":
        vals = np.ascontiguousarray(words).view(ml_dtypes.float8_e4m3fn).astype(np.float64)
    else:
        nib = np.empty((g, p, n, 4), np.uint8)
        nib[..., 0::2] = words & 0xF
        nib[..., 1::2] = words >> 4
        vals = E2M1[nib]
    vals = vals * np.repeat(np.exp2(scales.astype(np.float64) - 127.0), 8, axis=1)[..., None]
    return vals.transpose(0, 1, 3, 2).reshape(g * 512, n)

def pack4(w):
    words, scales = pack_weight(w, "e2m1")
    return words.reshape(words.shape[0], 128, -1), scales


def unpack4(words, scales):
    return unpack_weight(words.reshape(words.shape[0], 128, -1, 2), scales, "e2m1")


B, D_IN, D_H, W_RANK, U_RANK = 1024, 1024, 2048, 512, 512


def sigmoid(v):
    return 1.0 / (1.0 + np.exp(-v))


def setup_inputs():
    s, t = mx_kscale(W_RANK), mx_kscale(U_RANK)
    wx_r = bf(np.random.standard_normal((B, W_RANK)) * s)
    uh_r = bf(np.random.standard_normal((B, U_RANK)) * t)
    state = bf(np.random.standard_normal((B, D_H)))
    W2 = np.random.standard_normal((D_H, W_RANK)) * 0.7 / np.sqrt(W_RANK) / s
    U2 = np.random.standard_normal((D_H, U_RANK)) * 0.7 / np.sqrt(U_RANK) / t
    W2_words, W2_scales = pack4(np.ascontiguousarray(W2.T))
    U2_words, U2_scales = pack4(np.ascontiguousarray(U2.T))
    return {
        "wx_r": wx_r,
        "uh_r": uh_r,
        "state": state,
        "W2_words": W2_words,
        "W2_scales": W2_scales,
        "U2_words": U2_words,
        "U2_scales": U2_scales,
        "bias_gate": bf(1.0 + 0.5 * np.random.standard_normal((1, D_H))),
        "bias_update": bf(1.0 + 0.5 * np.random.standard_normal((1, D_H))),
        "zeta": bf(1.0 + 0.1 * np.random.standard_normal((1, 1))),
        "nu": bf(-1.5 + 0.1 * np.random.standard_normal((1, 1))),
    }


def reference(wx_r, uh_r, state, W2_words, W2_scales, U2_words, U2_scales, bias_gate, bias_update, zeta, nu):
    wx = mxq(f64(wx_r), 1, "e4m3") @ unpack4(W2_words, W2_scales)
    uh = mxq(f64(uh_r), 1, "e4m3") @ unpack4(U2_words, U2_scales)
    pre = wx + uh
    z = sigmoid(pre + f64(bias_gate))
    h_cand = np.tanh(pre + f64(bias_update))
    return z * f64(state) + (sigmoid(f64(zeta)) * (1.0 - z) + sigmoid(f64(nu))) * h_cand

@@ -1,0 +1,215 @@
+from contextlib import ExitStack
+
+import concourse.mybir as mybir
+from concourse.masks import make_identity
+
+F32 = mybir.dt.float32
+BF16 = mybir.dt.bfloat16
+I32 = mybir.dt.int32
+U32 = mybir.dt.uint32
+U8 = mybir.dt.uint8
+FP8X4 = mybir.dt.float8_e4m3fn_x4
+FP4X4 = mybir.dt.float4_e2m1fn_x4
+ACT = mybir.ActivationFunctionType
+ALU = mybir.AluOpType
+
+P = 128
+BATCH, RANK, HIDDEN = 1024, 512, 2048
+CHUNK = 512
+ROWS = CHUNK // P
+N_CHUNKS = BATCH // CHUNK
+N_BLOCKS = HIDDEN // P
+N_UNITS = N_CHUNKS * N_BLOCKS
+STORE_BLOCKS = 4
+PREPARE_STEPS = 6
+PREPARE_AT = 4
+
+FLOPS = 2 * BATCH * HIDDEN * 2 * RANK
+
+
+def tile_fastgrnncudacell_pa_kernel(
+    tc, wx_r, uh_r, state, W2_words, W2_scales, U2_words, U2_scales,
+    bias_gate, bias_update, zeta, nu, out,
+):
+    nc = tc.nc
+    with ExitStack() as ctx:
+        keep = ctx.enter_context(tc.tile_pool(name="keep", bufs=1))
+        work = ctx.enter_context(tc.tile_pool(name="work", bufs=3))
+        psum_pre = ctx.enter_context(tc.psum_pool(name="psum_pre", bufs=2))
+        psum_bank = ctx.enter_context(tc.psum_pool(name="psum_bank", bufs=6))
+        ctx.enter_context(tc.manual_schedule())
+
+        acts_dram = [x.rearrange("(c p b) k -> c p (b k)", p=P, b=ROWS) for x in (wx_r, uh_r)]
+        state_dram = state.rearrange("(c p b) n -> c p (b n)", p=P, b=ROWS)
+        out_dram = out.rearrange("(c p b) n -> c p b n", p=P, b=ROWS)
+
+        ident = keep.tile([P, P], F32)
+        acts = [[keep.tile([P, ROWS * RANK], BF16, name="acts%d%d" % (op, c))
+                 for c in range(N_CHUNKS)] for op in range(2)]
+        grouped = [[keep.tile([P, 4 * CHUNK], BF16, name="grouped%d%d" % (op, c), align_bytes=64)
+                    for c in range(N_CHUNKS)] for op in range(2)]
+        act_codes = keep.tile([P, 2, BATCH], U32, align_bytes=64)
+        act_scales = keep.tile([P, 2, BATCH], U8, align_bytes=64)
+        w_words = keep.tile([P, 2, 2 * HIDDEN], U8, align_bytes=64)
+        w_scales = keep.tile([P, 2, HIDDEN], U8, align_bytes=64)
+        state_sb = keep.tile([P, N_CHUNKS, ROWS, HIDDEN], BF16)
+        out_sb = keep.tile([P, N_CHUNKS, ROWS, HIDDEN], F32)
+        bias_rows = keep.tile([P, P], BF16)
+        bias_rows_f32 = keep.tile([P, P], F32)
+        bias_cols = keep.tile([P, 2 * N_BLOCKS], F32)
+        zeta_sb = keep.tile([P, 1], BF16)
+        nu_sb = keep.tile([P, 1], BF16)
+        sig_zeta = keep.tile([P, 1], F32)
+        sig_nu = keep.tile([P, 1], F32)
+        neg_sig_zeta = keep.tile([P, 1], F32)
+        sig_sum = keep.tile([P, 1], F32)
+
+        nc.vector.memset(w_scales[:].rearrange("p w n -> p (w n)").bitcast(I32), 0)
+        nc.vector.memset(bias_rows[:], 0.0)
+        make_identity(nc, ident[:])
+
+        for op in range(2):
+            nc.sync.dma_start(out=acts[op][0][:], in_=acts_dram[op][0])
+        for op, scales in enumerate((W2_scales, U2_scales)):
+            for quad in range(4):
+                nc.sync.dma_start(
+                    out=w_scales[32 * quad : 32 * quad + 4, op, :].bitcast(I32),
+                    in_=scales[0, 4 * quad : 4 * quad + 4, :].bitcast(I32),
+                )
+        for op, words in enumerate((W2_words, U2_words)):
+            nc.sync.dma_start(out=w_words[:, op, :].bitcast(I32), in_=words[0].bitcast(I32))
+        nc.sync.dma_start(out=state_sb[:, 0].rearrange("p b n -> p (b n)"), in_=state_dram[0])
+        for op in range(2):
+            nc.sync.dma_start(out=acts[op][1][:], in_=acts_dram[op][1])
+        nc.sync.dma_start(out=state_sb[:, 1].rearrange("p b n -> p (b n)"), in_=state_dram[1])
+
+        nc.scalar.dma_start(out=zeta_sb[:], in_=zeta.rearrange("a b -> (a b)").partition_broadcast(P))
+        nc.scalar.dma_start(out=nu_sb[:], in_=nu.rearrange("a b -> (a b)").partition_broadcast(P))
+        nc.scalar.dma_start(out=bias_rows[0:N_BLOCKS, :],
+                            in_=bias_gate.rearrange("o (d j) -> (o d) j", j=P))
+        nc.scalar.dma_start(out=bias_rows[N_BLOCKS : 2 * N_BLOCKS, :],
+                            in_=bias_update.rearrange("o (d j) -> (o d) j", j=P))
+
+        nc.scalar.activation(out=sig_zeta[:], in_=zeta_sb[:], func=ACT.Sigmoid)
+        nc.scalar.activation(out=sig_nu[:], in_=nu_sb[:], func=ACT.Sigmoid)
+        nc.vector.tensor_copy(out=bias_rows_f32[:], in_=bias_rows[:])
+
+        def prepare_step(c, step):
+            if step < 4:
+                op, half = step // 2, step % 2
+                words = acts[op][c][:].bitcast(F32).rearrange("p (b w) -> p b w", b=ROWS)
+                flipped = psum_bank.tile([P, 2, 2 * P], F32, tag="bank")
+                for i in range(2):
+                    for u in range(2):
+                        nc.tensor.transpose(
+                            out=flipped[:, u, i * P : (i + 1) * P],
+                            in_=words[:, 2 * half + i, u : RANK // 2 : 2],
+                            identity=ident[:],
+                        )
+                pairs = grouped[op][c][:].bitcast(F32).rearrange("p (n u) -> p n u", u=2)
+                target = pairs[:, half * 2 * P : (half + 1) * 2 * P, :]
+                source = flipped[:].rearrange("p u n -> p n u")
+                if c == 0 and half == 0:
+                    nc.vector.tensor_copy(out=target, in_=source)
+                else:
+                    nc.scalar.copy(out=target, in_=source)
+            else:
+                op = step - 4
+                cols = slice(c * CHUNK, (c + 1) * CHUNK)
+                nc.vector.quantize_mx(
+                    out=act_codes[:, op, cols].bitcast(FP8X4),
+                    scales=act_scales[:, op, cols],
+                    in_=grouped[op][c][:],
+                )
+
+        for step in range(4):
+            prepare_step(0, step)
+
+        bias_flipped = psum_bank.tile([P, P], F32, tag="bank")
+        nc.tensor.transpose(out=bias_flipped[:], in_=bias_rows_f32[:], identity=ident[:])
+        nc.vector.tensor_copy(out=bias_cols[:], in_=bias_flipped[:, 0 : 2 * N_BLOCKS])
+
+        for step in range(4, PREPARE_STEPS):
+            prepare_step(0, step)
+
+        nc.vector.tensor_scalar_mul(out=neg_sig_zeta[:], in0=sig_zeta[:], scalar1=-1.0)
+        nc.vector.tensor_add(out=sig_sum[:], in0=sig_zeta[:], in1=sig_nu[:])
+
+        pre_of, hidden_major, batch_major, partial = {}, {}, {}, {}
+
+        def multiply(u):
+            c, d = divmod(u, N_BLOCKS)
+            cols = slice(c * CHUNK, (c + 1) * CHUNK)
+            pre = psum_pre.tile([P, CHUNK], F32)
+            for op in range(2):
+                nc.tensor.matmul_mx(
+                    out=pre[:],
+                    lhsT=w_words[:, op, 2 * d * P : 2 * (d + 1) * P].bitcast(FP4X4),
+                    lhsT_scale=w_scales[:, op, d * P : (d + 1) * P],
+                    rhs=act_codes[:, op, cols].bitcast(FP8X4),
+                    rhs_scale=act_scales[:, op, cols],
+                    start=(op == 0),
+                    stop=(op == 1),
+                )
+            pre_of[u] = pre
+
+        def activate(u):
+            d = u % N_BLOCKS
+            cand_t = work.tile([P, CHUNK], F32)
+            gate_t = work.tile([P, CHUNK], F32)
+            nc.scalar.activation(out=cand_t[:], in_=pre_of[u][:], func=ACT.Tanh,
+                                 bias=bias_cols[:, N_BLOCKS + d : N_BLOCKS + d + 1])
+            nc.scalar.activation(out=gate_t[:], in_=pre_of[u][:], func=ACT.Sigmoid,
+                                 bias=bias_cols[:, d : d + 1])
+            hidden_major[u] = (cand_t, gate_t)
+
+        def flip_back(u):
+            flipped = []
+            for source in hidden_major[u]:
+                bank = psum_bank.tile([P, ROWS, P], F32, tag="bank")
+                for b in range(ROWS):
+                    nc.tensor.transpose(out=bank[:, b, :], in_=source[:, b * P : (b + 1) * P],
+                                        identity=ident[:])
+                flipped.append(bank)
+            batch_major[u] = flipped
+
+        def mix_1(u):
+            c, d = divmod(u, N_BLOCKS)
+            cand = batch_major[u][0]
+            rest = work.tile([P, ROWS, P], F32)
+            nc.vector.scalar_tensor_tensor(
+                out=rest[:], in0=cand[:], scalar=neg_sig_zeta[:, 0:1],
+                in1=state_sb[:, c, :, d * P : (d + 1) * P], op0=ALU.mult, op1=ALU.add)
+            partial[u] = rest
+
+        def mix_2(u):
+            gate = batch_major[u][1]
+            gated = work.tile([P, ROWS, P], F32)
+            nc.vector.tensor_tensor(out=gated[:], in0=partial[u][:], in1=gate[:], op=ALU.mult)
+            partial[u] = gated
+
+        def mix_3(u):
+            c, d = divmod(u, N_BLOCKS)
+            cand = batch_major[u][0]
+            nc.vector.scalar_tensor_tensor(
+                out=out_sb[:, c, :, d * P : (d + 1) * P], in0=cand[:], scalar=sig_sum[:, 0:1],
+                in1=partial[u][:], op0=ALU.mult, op1=ALU.add)
+            if (d + 1) % STORE_BLOCKS == 0:
+                cols = slice((d + 1 - STORE_BLOCKS) * P, (d + 1) * P)
+                nc.sync.dma_start(out=out_dram[c][:, :, cols], in_=out_sb[:, c, :, cols])
+
+        multiply(0)
+        activate(0)
+        for u in range(N_UNITS):
+            if u + 1 < N_UNITS:
+                multiply(u + 1)
+            flip_back(u)
+            if 0 <= u - PREPARE_AT < PREPARE_STEPS:
+                prepare_step(1, u - PREPARE_AT)
+            if u + 1 < N_UNITS:
+                activate(u + 1)
+            mix_1(u)
+            if u > 0:
+                mix_3(u - 1)
+            mix_2(u)
+        mix_3(N_UNITS - 1)

@@ -19,12 +19,17 @@ CHUNK = 512
 ROWS = CHUNK // P
 N_CHUNKS = BATCH // CHUNK
 N_BLOCKS = HIDDEN // P
-N_UNITS = N_CHUNKS * N_BLOCKS
-STORE_BLOCKS = 4
+ROUNDS_PER_CHUNK = N_BLOCKS // 2
+N_ROUNDS = N_CHUNKS * ROUNDS_PER_CHUNK
+AHEAD = 2
 PREPARE_STEPS = 6
-PREPARE_AT = 4
 
 FLOPS = 2 * BATCH * HIDDEN * 2 * RANK
+
+
+def place(r):
+    chunk, pair = divmod(r, ROUNDS_PER_CHUNK)
+    return chunk, 2 * pair, 2 * pair + 1
 
 
 def tile_fastgrnncudacell_pa_kernel(
@@ -34,20 +39,24 @@ def tile_fastgrnncudacell_pa_kernel(
     nc = tc.nc
     with ExitStack() as ctx:
         keep = ctx.enter_context(tc.tile_pool(name="keep", bufs=1))
-        work = ctx.enter_context(tc.tile_pool(name="work", bufs=3))
-        psum_pre = ctx.enter_context(tc.psum_pool(name="psum_pre", bufs=2))
-        psum_bank = ctx.enter_context(tc.psum_pool(name="psum_bank", bufs=6))
+        hidden_major = ctx.enter_context(tc.tile_pool(name="hidden_major", bufs=3 * 2))
+        helped_pool = ctx.enter_context(tc.tile_pool(name="helped_pool", bufs=3))
+        mixing = ctx.enter_context(tc.tile_pool(name="mixing", bufs=2))
+        psum_front = ctx.enter_context(tc.psum_pool(name="psum_front", bufs=3))
+        psum_twice = ctx.enter_context(tc.psum_pool(name="psum_twice", bufs=2))
+        psum_once = ctx.enter_context(tc.psum_pool(name="psum_once", bufs=3))
         ctx.enter_context(tc.manual_schedule())
 
         acts_dram = [x.rearrange("(c p b) k -> c p (b k)", p=P, b=ROWS) for x in (wx_r, uh_r)]
-        state_dram = state.rearrange("(c p b) n -> c p (b n)", p=P, b=ROWS)
+        state_dram = state.rearrange("(c p b) n -> c p b n", p=P, b=ROWS)
         out_dram = out.rearrange("(c p b) n -> c p b n", p=P, b=ROWS)
 
         ident = keep.tile([P, P], F32)
-        acts = [[keep.tile([P, ROWS * RANK], BF16, name="acts%d%d" % (op, c))
-                 for c in range(N_CHUNKS)] for op in range(2)]
-        grouped = [[keep.tile([P, 4 * CHUNK], BF16, name="grouped%d%d" % (op, c), align_bytes=64)
-                    for c in range(N_CHUNKS)] for op in range(2)]
+        acts = [[keep.tile([P, ROWS * RANK], BF16, name="acts%d%d" % (op, chunk))
+                 for chunk in range(N_CHUNKS)] for op in range(2)]
+        grouped = [[keep.tile([P, 4 * CHUNK], BF16, name="grouped%d%d" % (op, chunk),
+                              align_bytes=64)
+                    for chunk in range(N_CHUNKS)] for op in range(2)]
         act_codes = keep.tile([P, 2, BATCH], U32, align_bytes=64)
         act_scales = keep.tile([P, 2, BATCH], U8, align_bytes=64)
         w_words = keep.tile([P, 2, 2 * HIDDEN], U8, align_bytes=64)
@@ -68,8 +77,17 @@ def tile_fastgrnncudacell_pa_kernel(
         nc.vector.memset(bias_rows[:], 0.0)
         make_identity(nc, ident[:])
 
-        for op in range(2):
-            nc.sync.dma_start(out=acts[op][0][:], in_=acts_dram[op][0])
+        def load_acts(chunk):
+            for op in range(2):
+                for half in range(2):
+                    cols = slice(half * 2 * RANK, (half + 1) * 2 * RANK)
+                    nc.sync.dma_start(out=acts[op][chunk][:, cols], in_=acts_dram[op][chunk][:, cols])
+
+        def load_state(chunk, half):
+            cols = slice(half * HIDDEN // 2, (half + 1) * HIDDEN // 2)
+            nc.sync.dma_start(out=state_sb[:, chunk, :, cols], in_=state_dram[chunk][:, :, cols])
+
+        load_acts(0)
         for op, scales in enumerate((W2_scales, U2_scales)):
             for quad in range(4):
                 nc.sync.dma_start(
@@ -78,10 +96,11 @@ def tile_fastgrnncudacell_pa_kernel(
                 )
         for op, words in enumerate((W2_words, U2_words)):
             nc.sync.dma_start(out=w_words[:, op, :].bitcast(I32), in_=words[0].bitcast(I32))
-        nc.sync.dma_start(out=state_sb[:, 0].rearrange("p b n -> p (b n)"), in_=state_dram[0])
-        for op in range(2):
-            nc.sync.dma_start(out=acts[op][1][:], in_=acts_dram[op][1])
-        nc.sync.dma_start(out=state_sb[:, 1].rearrange("p b n -> p (b n)"), in_=state_dram[1])
+        load_state(0, 0)
+        load_acts(1)
+        load_state(0, 1)
+        load_state(1, 0)
+        load_state(1, 1)
 
         nc.scalar.dma_start(out=zeta_sb[:], in_=zeta.rearrange("a b -> (a b)").partition_broadcast(P))
         nc.scalar.dma_start(out=nu_sb[:], in_=nu.rearrange("a b -> (a b)").partition_broadcast(P))
@@ -94,38 +113,38 @@ def tile_fastgrnncudacell_pa_kernel(
         nc.scalar.activation(out=sig_nu[:], in_=nu_sb[:], func=ACT.Sigmoid)
         nc.vector.tensor_copy(out=bias_rows_f32[:], in_=bias_rows[:])
 
-        def prepare_step(c, step):
+        def prepare_step(chunk, step):
             if step < 4:
                 op, half = step // 2, step % 2
-                words = acts[op][c][:].bitcast(F32).rearrange("p (b w) -> p b w", b=ROWS)
-                flipped = psum_bank.tile([P, 2, 2 * P], F32, tag="bank")
+                words = acts[op][chunk][:].bitcast(F32).rearrange("p (b w) -> p b w", b=ROWS)
+                halves = psum_front.tile([P, 2, 2 * P], F32, tag="front")
                 for i in range(2):
                     for u in range(2):
                         nc.tensor.transpose(
-                            out=flipped[:, u, i * P : (i + 1) * P],
+                            out=halves[:, u, i * P : (i + 1) * P],
                             in_=words[:, 2 * half + i, u : RANK // 2 : 2],
                             identity=ident[:],
                         )
-                pairs = grouped[op][c][:].bitcast(F32).rearrange("p (n u) -> p n u", u=2)
+                pairs = grouped[op][chunk][:].bitcast(F32).rearrange("p (n u) -> p n u", u=2)
                 target = pairs[:, half * 2 * P : (half + 1) * 2 * P, :]
-                source = flipped[:].rearrange("p u n -> p n u")
-                if c == 0 and half == 0:
+                source = halves[:].rearrange("p u n -> p n u")
+                if chunk == 0 and half == 0:
                     nc.vector.tensor_copy(out=target, in_=source)
                 else:
                     nc.scalar.copy(out=target, in_=source)
             else:
                 op = step - 4
-                cols = slice(c * CHUNK, (c + 1) * CHUNK)
+                cols = slice(chunk * CHUNK, (chunk + 1) * CHUNK)
                 nc.vector.quantize_mx(
                     out=act_codes[:, op, cols].bitcast(FP8X4),
                     scales=act_scales[:, op, cols],
-                    in_=grouped[op][c][:],
+                    in_=grouped[op][chunk][:],
                 )
 
         for step in range(4):
             prepare_step(0, step)
 
-        bias_flipped = psum_bank.tile([P, P], F32, tag="bank")
+        bias_flipped = psum_front.tile([P, P], F32, tag="front")
         nc.tensor.transpose(out=bias_flipped[:], in_=bias_rows_f32[:], identity=ident[:])
         nc.vector.tensor_copy(out=bias_cols[:], in_=bias_flipped[:, 0 : 2 * N_BLOCKS])
 
@@ -135,81 +154,117 @@ def tile_fastgrnncudacell_pa_kernel(
         nc.vector.tensor_scalar_mul(out=neg_sig_zeta[:], in0=sig_zeta[:], scalar1=-1.0)
         nc.vector.tensor_add(out=sig_sum[:], in0=sig_zeta[:], in1=sig_nu[:])
 
-        pre_of, hidden_major, batch_major, partial = {}, {}, {}, {}
+        products, transposed, banks, sums = {}, {}, {}, {}
 
-        def multiply(u):
-            c, d = divmod(u, N_BLOCKS)
-            cols = slice(c * CHUNK, (c + 1) * CHUNK)
-            pre = psum_pre.tile([P, CHUNK], F32)
-            for op in range(2):
-                nc.tensor.matmul_mx(
-                    out=pre[:],
-                    lhsT=w_words[:, op, 2 * d * P : 2 * (d + 1) * P].bitcast(FP4X4),
-                    lhsT_scale=w_scales[:, op, d * P : (d + 1) * P],
-                    rhs=act_codes[:, op, cols].bitcast(FP8X4),
-                    rhs_scale=act_scales[:, op, cols],
-                    start=(op == 0),
-                    stop=(op == 1),
-                )
-            pre_of[u] = pre
+        def multiply(r):
+            chunk, plain, helped = place(r)
+            cols = slice(chunk * CHUNK, (chunk + 1) * CHUNK)
+            for d in (helped, plain):
+                pre = psum_front.tile([P, CHUNK], F32, tag="front")
+                for op in range(2):
+                    nc.tensor.matmul_mx(
+                        out=pre[:],
+                        lhsT=w_words[:, op, 2 * d * P : 2 * (d + 1) * P].bitcast(FP4X4),
+                        lhsT_scale=w_scales[:, op, d * P : (d + 1) * P],
+                        rhs=act_codes[:, op, cols].bitcast(FP8X4),
+                        rhs_scale=act_scales[:, op, cols],
+                        start=(op == 0),
+                        stop=(op == 1),
+                    )
+                products[d, chunk] = pre
 
-        def activate(u):
-            d = u % N_BLOCKS
-            cand_t = work.tile([P, CHUNK], F32)
-            gate_t = work.tile([P, CHUNK], F32)
-            nc.scalar.activation(out=cand_t[:], in_=pre_of[u][:], func=ACT.Tanh,
-                                 bias=bias_cols[:, N_BLOCKS + d : N_BLOCKS + d + 1])
-            nc.scalar.activation(out=gate_t[:], in_=pre_of[u][:], func=ACT.Sigmoid,
+        def gate_of(pre, d):
+            gate_t = hidden_major.tile([P, CHUNK], F32)
+            nc.scalar.activation(out=gate_t[:], in_=pre[:], func=ACT.Sigmoid,
                                  bias=bias_cols[:, d : d + 1])
-            hidden_major[u] = (cand_t, gate_t)
+            return gate_t
 
-        def flip_back(u):
-            flipped = []
-            for source in hidden_major[u]:
-                bank = psum_bank.tile([P, ROWS, P], F32, tag="bank")
-                for b in range(ROWS):
-                    nc.tensor.transpose(out=bank[:, b, :], in_=source[:, b * P : (b + 1) * P],
-                                        identity=ident[:])
-                flipped.append(bank)
-            batch_major[u] = flipped
+        def candidate_of(pre, d):
+            cand_t = hidden_major.tile([P, CHUNK], F32)
+            nc.scalar.activation(out=cand_t[:], in_=pre[:], func=ACT.Tanh,
+                                 bias=bias_cols[:, N_BLOCKS + d : N_BLOCKS + d + 1])
+            return cand_t
 
-        def mix_1(u):
-            c, d = divmod(u, N_BLOCKS)
-            cand = batch_major[u][0]
-            rest = work.tile([P, ROWS, P], F32)
+        def activate(r):
+            chunk, plain, helped = place(r)
+            gate_helped = gate_of(products[helped, chunk], helped)
+            cand_helped = candidate_of(products[helped, chunk], helped)
+            cand_plain = candidate_of(products[plain, chunk], plain)
+            gate_plain = gate_of(products[plain, chunk], plain)
+            weight_t = helped_pool.tile([P, CHUNK], F32)
+            nc.gpsimd.tensor_scalar(out=weight_t[:], in0=gate_helped[:],
+                                    scalar1=neg_sig_zeta[:, 0:1], scalar2=sig_sum[:, 0:1],
+                                    op0=ALU.mult, op1=ALU.add)
+            fresh_t = helped_pool.tile([P, CHUNK], F32)
+            nc.gpsimd.tensor_tensor(out=fresh_t[:], in0=weight_t[:], in1=cand_helped[:], op=ALU.mult)
+            transposed[r] = (gate_helped, cand_plain, gate_plain, fresh_t)
+
+        def flip_back(source, pool):
+            bank = pool.tile([P, ROWS, P], F32)
+            for b in range(ROWS):
+                nc.tensor.transpose(out=bank[:, b, :], in_=source[:, b * P : (b + 1) * P],
+                                    identity=ident[:])
+            return bank
+
+        def flip_round(r):
+            gate_helped, cand_plain, gate_plain, fresh_t = transposed[r]
+            banks[r] = (flip_back(gate_helped, psum_once), flip_back(cand_plain, psum_twice),
+                        flip_back(gate_plain, psum_once), flip_back(fresh_t, psum_once))
+
+        def state_of(chunk, d):
+            return state_sb[:, chunk, :, d * P : (d + 1) * P]
+
+        def out_of(chunk, d):
+            return out_sb[:, chunk, :, d * P : (d + 1) * P]
+
+        def helped_1(r):
+            chunk, plain, helped = place(r)
+            kept = mixing.tile([P, ROWS, P], F32)
+            nc.vector.tensor_tensor(out=kept[:], in0=banks[r][0][:], in1=state_of(chunk, helped),
+                                    op=ALU.mult)
+            sums[r, "kept"] = kept
+
+        def helped_2(r):
+            chunk, plain, helped = place(r)
+            nc.vector.tensor_tensor(out=out_of(chunk, helped), in0=banks[r][3][:],
+                                    in1=sums[r, "kept"][:], op=ALU.add)
+
+        def plain_1(r):
+            chunk, plain, helped = place(r)
+            rest = mixing.tile([P, ROWS, P], F32)
             nc.vector.scalar_tensor_tensor(
-                out=rest[:], in0=cand[:], scalar=neg_sig_zeta[:, 0:1],
-                in1=state_sb[:, c, :, d * P : (d + 1) * P], op0=ALU.mult, op1=ALU.add)
-            partial[u] = rest
+                out=rest[:], in0=banks[r][1][:], scalar=neg_sig_zeta[:, 0:1],
+                in1=state_of(chunk, plain), op0=ALU.mult, op1=ALU.add)
+            sums[r, "rest"] = rest
 
-        def mix_2(u):
-            gate = batch_major[u][1]
-            gated = work.tile([P, ROWS, P], F32)
-            nc.vector.tensor_tensor(out=gated[:], in0=partial[u][:], in1=gate[:], op=ALU.mult)
-            partial[u] = gated
+        def plain_2(r):
+            gated = mixing.tile([P, ROWS, P], F32)
+            nc.vector.tensor_tensor(out=gated[:], in0=sums[r, "rest"][:], in1=banks[r][2][:],
+                                    op=ALU.mult)
+            sums[r, "gated"] = gated
 
-        def mix_3(u):
-            c, d = divmod(u, N_BLOCKS)
-            cand = batch_major[u][0]
+        def plain_3_and_store(r):
+            chunk, plain, helped = place(r)
             nc.vector.scalar_tensor_tensor(
-                out=out_sb[:, c, :, d * P : (d + 1) * P], in0=cand[:], scalar=sig_sum[:, 0:1],
-                in1=partial[u][:], op0=ALU.mult, op1=ALU.add)
-            if (d + 1) % STORE_BLOCKS == 0:
-                cols = slice((d + 1 - STORE_BLOCKS) * P, (d + 1) * P)
-                nc.sync.dma_start(out=out_dram[c][:, :, cols], in_=out_sb[:, c, :, cols])
+                out=out_of(chunk, plain), in0=banks[r][1][:], scalar=sig_sum[:, 0:1],
+                in1=sums[r, "gated"][:], op0=ALU.mult, op1=ALU.add)
+            cols = slice(plain * P, (helped + 1) * P)
+            nc.sync.dma_start(out=out_dram[chunk][:, :, cols], in_=out_sb[:, chunk, :, cols])
 
-        multiply(0)
-        activate(0)
-        for u in range(N_UNITS):
-            if u + 1 < N_UNITS:
-                multiply(u + 1)
-            flip_back(u)
-            if 0 <= u - PREPARE_AT < PREPARE_STEPS:
-                prepare_step(1, u - PREPARE_AT)
-            if u + 1 < N_UNITS:
-                activate(u + 1)
-            mix_1(u)
-            if u > 0:
-                mix_3(u - 1)
-            mix_2(u)
-        mix_3(N_UNITS - 1)
+        for r in range(AHEAD):
+            multiply(r)
+            activate(r)
+        for r in range(N_ROUNDS):
+            flip_round(r)
+            if r < PREPARE_STEPS:
+                prepare_step(1, r)
+            if r + AHEAD < N_ROUNDS:
+                multiply(r + AHEAD)
+                activate(r + AHEAD)
+            helped_1(r)
+            plain_1(r)
+            if r > 0:
+                plain_3_and_store(r - 1)
+            plain_2(r)
+            helped_2(r)
+        plain_3_and_store(N_ROUNDS - 1)

@@ -22,7 +22,8 @@ N_BLOCKS = HIDDEN // P
 ROUNDS_PER_CHUNK = N_BLOCKS // 2
 N_ROUNDS = N_CHUNKS * ROUNDS_PER_CHUNK
 AHEAD = 2
-PREPARE_STEPS = 6
+PREPARE_BANKS = 4
+PREPARE_STEPS = PREPARE_BANKS + 1
 
 FLOPS = 2 * BATCH * HIDDEN * 2 * RANK
 
@@ -113,43 +114,48 @@ def tile_fastgrnncudacell_pa_kernel(
         nc.scalar.activation(out=sig_nu[:], in_=nu_sb[:], func=ACT.Sigmoid)
         nc.vector.tensor_copy(out=bias_rows_f32[:], in_=bias_rows[:])
 
-        def prepare_step(chunk, step):
-            if step < 4:
-                op, half = step // 2, step % 2
-                words = acts[op][chunk][:].bitcast(F32).rearrange("p (b w) -> p b w", b=ROWS)
-                halves = psum_front.tile([P, 2, 2 * P], F32, tag="front")
-                for i in range(2):
-                    for u in range(2):
-                        nc.tensor.transpose(
-                            out=halves[:, u, i * P : (i + 1) * P],
-                            in_=words[:, 2 * half + i, u : RANK // 2 : 2],
-                            identity=ident[:],
-                        )
-                pairs = grouped[op][chunk][:].bitcast(F32).rearrange("p (n u) -> p n u", u=2)
-                target = pairs[:, half * 2 * P : (half + 1) * 2 * P, :]
-                source = halves[:].rearrange("p u n -> p n u")
-                if chunk == 0 and half == 0:
-                    nc.vector.tensor_copy(out=target, in_=source)
-                else:
-                    nc.scalar.copy(out=target, in_=source)
+        def flip_and_copy(chunk, quarter):
+            op, half = divmod(quarter, 2)
+            words = acts[op][chunk][:].bitcast(F32).rearrange("p (b w) -> p b w", b=ROWS)
+            halves = psum_front.tile([P, 2, 2 * P], F32, tag="front")
+            for i in range(2):
+                for u in range(2):
+                    nc.tensor.transpose(
+                        out=halves[:, u, i * P : (i + 1) * P],
+                        in_=words[:, 2 * half + i, u : RANK // 2 : 2],
+                        identity=ident[:],
+                    )
+            pairs = grouped[op][chunk][:].bitcast(F32).rearrange("p (n u) -> p n u", u=2)
+            target = pairs[:, half * 2 * P : (half + 1) * 2 * P, :]
+            source = halves[:].rearrange("p u n -> p n u")
+            if chunk == 0 and half == 0:
+                nc.vector.tensor_copy(out=target, in_=source)
             else:
-                op = step - 4
-                cols = slice(chunk * CHUNK, (chunk + 1) * CHUNK)
-                nc.vector.quantize_mx(
-                    out=act_codes[:, op, cols].bitcast(FP8X4),
-                    scales=act_scales[:, op, cols],
-                    in_=grouped[op][chunk][:],
-                )
+                nc.scalar.copy(out=target, in_=source)
 
-        for step in range(4):
+        def quantise(chunk, quarter):
+            op, half = divmod(quarter, 2)
+            first = chunk * CHUNK + half * 2 * P
+            nc.vector.quantize_mx(
+                out=act_codes[:, op, first : first + 2 * P].bitcast(FP8X4),
+                scales=act_scales[:, op, first : first + 2 * P],
+                in_=grouped[op][chunk][:, half * 8 * P : (half + 1) * 8 * P],
+            )
+
+        def prepare_step(chunk, step):
+            if step < PREPARE_BANKS:
+                flip_and_copy(chunk, step)
+            if step > 0:
+                quantise(chunk, step - 1)
+
+        for step in range(PREPARE_BANKS):
             prepare_step(0, step)
 
         bias_flipped = psum_front.tile([P, P], F32, tag="front")
         nc.tensor.transpose(out=bias_flipped[:], in_=bias_rows_f32[:], identity=ident[:])
         nc.vector.tensor_copy(out=bias_cols[:], in_=bias_flipped[:, 0 : 2 * N_BLOCKS])
 
-        for step in range(4, PREPARE_STEPS):
-            prepare_step(0, step)
+        prepare_step(0, PREPARE_BANKS)
 
         nc.vector.tensor_scalar_mul(out=neg_sig_zeta[:], in0=sig_zeta[:], scalar1=-1.0)
         nc.vector.tensor_add(out=sig_sum[:], in0=sig_zeta[:], in1=sig_nu[:])
@@ -217,6 +223,9 @@ def tile_fastgrnncudacell_pa_kernel(
         def out_of(chunk, d):
             return out_sb[:, chunk, :, d * P : (d + 1) * P]
 
+        def store(chunk, d):
+            nc.sync.dma_start(out=out_dram[chunk][:, :, d * P : (d + 1) * P], in_=out_of(chunk, d))
+
         def helped_1(r):
             chunk, plain, helped = place(r)
             kept = mixing.tile([P, ROWS, P], F32)
@@ -228,6 +237,7 @@ def tile_fastgrnncudacell_pa_kernel(
             chunk, plain, helped = place(r)
             nc.vector.tensor_tensor(out=out_of(chunk, helped), in0=banks[r][3][:],
                                     in1=sums[r, "kept"][:], op=ALU.add)
+            store(chunk, helped)
 
         def plain_1(r):
             chunk, plain, helped = place(r)
@@ -243,13 +253,12 @@ def tile_fastgrnncudacell_pa_kernel(
                                     op=ALU.mult)
             sums[r, "gated"] = gated
 
-        def plain_3_and_store(r):
+        def plain_3(r):
             chunk, plain, helped = place(r)
             nc.vector.scalar_tensor_tensor(
                 out=out_of(chunk, plain), in0=banks[r][1][:], scalar=sig_sum[:, 0:1],
                 in1=sums[r, "gated"][:], op0=ALU.mult, op1=ALU.add)
-            cols = slice(plain * P, (helped + 1) * P)
-            nc.sync.dma_start(out=out_dram[chunk][:, :, cols], in_=out_sb[:, chunk, :, cols])
+            store(chunk, plain)
 
         for r in range(AHEAD):
             multiply(r)
@@ -264,7 +273,7 @@ def tile_fastgrnncudacell_pa_kernel(
             helped_1(r)
             plain_1(r)
             if r > 0:
-                plain_3_and_store(r - 1)
+                plain_3(r - 1)
             plain_2(r)
             helped_2(r)
-        plain_3_and_store(N_ROUNDS - 1)
+        plain_3(N_ROUNDS - 1)

@@ -162,22 +162,28 @@ def tile_fastgrnncudacell_pa_kernel(
 
         products, transposed, banks, sums = {}, {}, {}, {}
 
-        def multiply(r):
-            chunk, plain, helped = place(r)
+        def multiply(chunk, d):
             cols = slice(chunk * CHUNK, (chunk + 1) * CHUNK)
-            for d in (helped, plain):
-                pre = psum_front.tile([P, CHUNK], F32, tag="front")
-                for op in range(2):
-                    nc.tensor.matmul_mx(
-                        out=pre[:],
-                        lhsT=w_words[:, op, 2 * d * P : 2 * (d + 1) * P].bitcast(FP4X4),
-                        lhsT_scale=w_scales[:, op, d * P : (d + 1) * P],
-                        rhs=act_codes[:, op, cols].bitcast(FP8X4),
-                        rhs_scale=act_scales[:, op, cols],
-                        start=(op == 0),
-                        stop=(op == 1),
-                    )
-                products[d, chunk] = pre
+            pre = psum_front.tile([P, CHUNK], F32, tag="front")
+            for op in range(2):
+                nc.tensor.matmul_mx(
+                    out=pre[:],
+                    lhsT=w_words[:, op, 2 * d * P : 2 * (d + 1) * P].bitcast(FP4X4),
+                    lhsT_scale=w_scales[:, op, d * P : (d + 1) * P],
+                    rhs=act_codes[:, op, cols].bitcast(FP8X4),
+                    rhs_scale=act_scales[:, op, cols],
+                    start=(op == 0),
+                    stop=(op == 1),
+                )
+            products[d, chunk] = pre
+
+        def multiply_helped(r):
+            chunk, plain, helped = place(r)
+            multiply(chunk, helped)
+
+        def multiply_plain(r):
+            chunk, plain, helped = place(r)
+            multiply(chunk, plain)
 
         def gate_of(pre, d):
             gate_t = hidden_major.tile([P, CHUNK], F32)
@@ -212,10 +218,13 @@ def tile_fastgrnncudacell_pa_kernel(
                                     identity=ident[:])
             return bank
 
-        def flip_round(r):
+        def flip_first_half(r):
             gate_helped, cand_plain, gate_plain, fresh_t = transposed[r]
-            banks[r] = (flip_back(gate_helped, psum_once), flip_back(cand_plain, psum_twice),
-                        flip_back(gate_plain, psum_once), flip_back(fresh_t, psum_once))
+            banks[r] = [flip_back(gate_helped, psum_once), flip_back(cand_plain, psum_twice)]
+
+        def flip_second_half(r):
+            gate_helped, cand_plain, gate_plain, fresh_t = transposed[r]
+            banks[r].extend([flip_back(gate_plain, psum_once), flip_back(fresh_t, psum_once)])
 
         def state_of(chunk, d):
             return state_sb[:, chunk, :, d * P : (d + 1) * P]
@@ -261,14 +270,18 @@ def tile_fastgrnncudacell_pa_kernel(
             store(chunk, plain)
 
         for r in range(AHEAD):
-            multiply(r)
+            multiply_helped(r)
+            multiply_plain(r)
             activate(r)
         for r in range(N_ROUNDS):
-            flip_round(r)
+            flip_first_half(r)
+            if r + AHEAD < N_ROUNDS:
+                multiply_helped(r + AHEAD)
+            flip_second_half(r)
             if r < PREPARE_STEPS:
                 prepare_step(1, r)
             if r + AHEAD < N_ROUNDS:
-                multiply(r + AHEAD)
+                multiply_plain(r + AHEAD)
                 activate(r + AHEAD)
             helped_1(r)
             plain_1(r)

@@ -84,9 +84,14 @@ def tile_fastgrnncudacell_pa_kernel(
                     cols = slice(half * 2 * RANK, (half + 1) * 2 * RANK)
                     nc.sync.dma_start(out=acts[op][chunk][:, cols], in_=acts_dram[op][chunk][:, cols])
 
-        def load_state(chunk, half):
-            cols = slice(half * HIDDEN // 2, (half + 1) * HIDDEN // 2)
+        def load_state(chunk, part):
+            cols = slice(part * HIDDEN // 4, (part + 1) * HIDDEN // 4)
             nc.sync.dma_start(out=state_sb[:, chunk, :, cols], in_=state_dram[chunk][:, :, cols])
+
+        def load_words(first_block, last_block):
+            cols = slice(2 * first_block * P, 2 * last_block * P)
+            for op, words in enumerate((W2_words, U2_words)):
+                nc.sync.dma_start(out=w_words[:, op, cols].bitcast(I32), in_=words[0][:, cols].bitcast(I32))
 
         load_acts(0)
         for op, scales in enumerate((W2_scales, U2_scales)):
@@ -95,13 +100,15 @@ def tile_fastgrnncudacell_pa_kernel(
                     out=w_scales[32 * quad : 32 * quad + 4, op, :].bitcast(I32),
                     in_=scales[0, 4 * quad : 4 * quad + 4, :].bitcast(I32),
                 )
-        for op, words in enumerate((W2_words, U2_words)):
-            nc.sync.dma_start(out=w_words[:, op, :].bitcast(I32), in_=words[0].bitcast(I32))
+        load_words(0, 4)
         load_state(0, 0)
-        load_acts(1)
+        load_words(4, N_BLOCKS)
         load_state(0, 1)
-        load_state(1, 0)
-        load_state(1, 1)
+        load_acts(1)
+        load_state(0, 2)
+        load_state(0, 3)
+        for part in range(4):
+            load_state(1, part)
 
         nc.scalar.dma_start(out=zeta_sb[:], in_=zeta.rearrange("a b -> (a b)").partition_broadcast(P))
         nc.scalar.dma_start(out=nu_sb[:], in_=nu.rearrange("a b -> (a b)").partition_broadcast(P))

@@ -28,9 +28,16 @@ PREPARE_STEPS = PREPARE_BANKS + 1
 FLOPS = 2 * BATCH * HIDDEN * 2 * RANK
 
 
+BOTH_HELPED = (2, 5)
+
+
 def place(r):
     chunk, pair = divmod(r, ROUNDS_PER_CHUNK)
-    return chunk, 2 * pair, 2 * pair + 1
+    return chunk, (2 * pair, 2 * pair + 1)
+
+
+def both_helped(r):
+    return (r % ROUNDS_PER_CHUNK) in BOTH_HELPED
 
 
 def tile_fastgrnncudacell_pa_kernel(
@@ -41,7 +48,7 @@ def tile_fastgrnncudacell_pa_kernel(
     with ExitStack() as ctx:
         keep = ctx.enter_context(tc.tile_pool(name="keep", bufs=1))
         hidden_major = ctx.enter_context(tc.tile_pool(name="hidden_major", bufs=3 * 2))
-        helped_pool = ctx.enter_context(tc.tile_pool(name="helped_pool", bufs=3))
+        helped_pool = ctx.enter_context(tc.tile_pool(name="helped_pool", bufs=4))
         mixing = ctx.enter_context(tc.tile_pool(name="mixing", bufs=2))
         psum_front = ctx.enter_context(tc.psum_pool(name="psum_front", bufs=3))
         psum_twice = ctx.enter_context(tc.psum_pool(name="psum_twice", bufs=2))
@@ -169,7 +176,9 @@ def tile_fastgrnncudacell_pa_kernel(
 
         products, transposed, banks, sums = {}, {}, {}, {}
 
-        def multiply(chunk, d):
+        def multiply(r, i):
+            chunk, blocks = place(r)
+            d = blocks[i]
             cols = slice(chunk * CHUNK, (chunk + 1) * CHUNK)
             pre = psum_front.tile([P, CHUNK], F32, tag="front")
             for op in range(2):
@@ -182,41 +191,60 @@ def tile_fastgrnncudacell_pa_kernel(
                     start=(op == 0),
                     stop=(op == 1),
                 )
-            products[d, chunk] = pre
-
-        def multiply_helped(r):
-            chunk, plain, helped = place(r)
-            multiply(chunk, helped)
-
-        def multiply_plain(r):
-            chunk, plain, helped = place(r)
-            multiply(chunk, plain)
-
-        def gate_of(pre, d):
-            gate_t = hidden_major.tile([P, CHUNK], F32)
-            nc.scalar.activation(out=gate_t[:], in_=pre[:], func=ACT.Sigmoid,
-                                 bias=bias_cols[:, d : d + 1])
-            return gate_t
-
-        def candidate_of(pre, d):
-            cand_t = hidden_major.tile([P, CHUNK], F32)
-            nc.scalar.activation(out=cand_t[:], in_=pre[:], func=ACT.Tanh,
-                                 bias=bias_cols[:, N_BLOCKS + d : N_BLOCKS + d + 1])
-            return cand_t
+            products[r, i] = pre
 
         def activate(r):
-            chunk, plain, helped = place(r)
-            gate_helped = gate_of(products[helped, chunk], helped)
-            cand_helped = candidate_of(products[helped, chunk], helped)
-            cand_plain = candidate_of(products[plain, chunk], plain)
-            gate_plain = gate_of(products[plain, chunk], plain)
-            weight_t = helped_pool.tile([P, CHUNK], F32)
-            nc.gpsimd.tensor_scalar(out=weight_t[:], in0=gate_helped[:],
-                                    scalar1=neg_sig_zeta[:, 0:1], scalar2=sig_sum[:, 0:1],
-                                    op0=ALU.mult, op1=ALU.add)
-            fresh_t = helped_pool.tile([P, CHUNK], F32)
-            nc.gpsimd.tensor_tensor(out=fresh_t[:], in0=weight_t[:], in1=cand_helped[:], op=ALU.mult)
-            transposed[r] = (gate_helped, cand_plain, gate_plain, fresh_t)
+            chunk, blocks = place(r)
+            gates, cands, fresh = {}, {}, {}
+
+            def gate_of(i):
+                d = blocks[i]
+                gate_t = hidden_major.tile([P, CHUNK], F32)
+                nc.scalar.activation(out=gate_t[:], in_=products[r, i][:], func=ACT.Sigmoid,
+                                     bias=bias_cols[:, d : d + 1])
+                gates[i] = gate_t
+
+            def candidate_of(i):
+                d = blocks[i]
+                cand_t = hidden_major.tile([P, CHUNK], F32)
+                nc.scalar.activation(out=cand_t[:], in_=products[r, i][:], func=ACT.Tanh,
+                                     bias=bias_cols[:, N_BLOCKS + d : N_BLOCKS + d + 1])
+                cands[i] = cand_t
+
+            weights = {}
+
+            def weight_of(i, on_scalar):
+                weight_t = helped_pool.tile([P, CHUNK], F32)
+                if on_scalar:
+                    nc.scalar.activation(out=weight_t[:], in_=gates[i][:], func=ACT.Identity,
+                                         scale=neg_sig_zeta[:, 0:1], bias=sig_sum[:, 0:1])
+                else:
+                    nc.gpsimd.tensor_scalar(out=weight_t[:], in0=gates[i][:],
+                                            scalar1=neg_sig_zeta[:, 0:1], scalar2=sig_sum[:, 0:1],
+                                            op0=ALU.mult, op1=ALU.add)
+                weights[i] = weight_t
+
+            def new_part_of(i):
+                weight_t = weights[i]
+                fresh_t = helped_pool.tile([P, CHUNK], F32)
+                nc.gpsimd.tensor_tensor(out=fresh_t[:], in0=weight_t[:], in1=cands[i][:], op=ALU.mult)
+                fresh[i] = fresh_t
+
+            gate_of(1)
+            candidate_of(1)
+            if both_helped(r):
+                weight_of(1, True)
+                new_part_of(1)
+                gate_of(0)
+                candidate_of(0)
+                weight_of(0, True)
+                new_part_of(0)
+            else:
+                candidate_of(0)
+                gate_of(0)
+                weight_of(1, False)
+                new_part_of(1)
+            transposed[r] = (gates, cands, fresh)
 
         def flip_back(source, pool):
             bank = pool.tile([P, ROWS, P], F32)
@@ -226,12 +254,20 @@ def tile_fastgrnncudacell_pa_kernel(
             return bank
 
         def flip_first_half(r):
-            gate_helped, cand_plain, gate_plain, fresh_t = transposed[r]
-            banks[r] = [flip_back(gate_helped, psum_once), flip_back(cand_plain, psum_twice)]
+            gate_t, cand_t, fresh_t = transposed[r]
+            if both_helped(r):
+                first = gate_t[0]
+            else:
+                first = cand_t[0]
+            second_bank = flip_back(gate_t[1], psum_once)
+            banks[r] = [flip_back(first, psum_twice), second_bank]
 
         def flip_second_half(r):
-            gate_helped, cand_plain, gate_plain, fresh_t = transposed[r]
-            banks[r].extend([flip_back(gate_plain, psum_once), flip_back(fresh_t, psum_once)])
+            gate_t, cand_t, fresh_t = transposed[r]
+            if both_helped(r):
+                banks[r].extend([flip_back(fresh_t[0], psum_once), flip_back(fresh_t[1], psum_once)])
+            else:
+                banks[r].extend([flip_back(gate_t[0], psum_once), flip_back(fresh_t[1], psum_once)])
 
         def state_of(chunk, d):
             return state_sb[:, chunk, :, d * P : (d + 1) * P]
@@ -242,25 +278,25 @@ def tile_fastgrnncudacell_pa_kernel(
         def store(chunk, d):
             nc.sync.dma_start(out=out_dram[chunk][:, :, d * P : (d + 1) * P], in_=out_of(chunk, d))
 
-        def helped_1(r):
-            chunk, plain, helped = place(r)
+        def helped_1(r, i):
+            chunk, blocks = place(r)
             kept = mixing.tile([P, ROWS, P], F32)
-            nc.vector.tensor_tensor(out=kept[:], in0=banks[r][0][:], in1=state_of(chunk, helped),
+            nc.vector.tensor_tensor(out=kept[:], in0=banks[r][i][:], in1=state_of(chunk, blocks[i]),
                                     op=ALU.mult)
-            sums[r, "kept"] = kept
+            sums[r, "kept", i] = kept
 
-        def helped_2(r):
-            chunk, plain, helped = place(r)
-            nc.vector.tensor_tensor(out=out_of(chunk, helped), in0=banks[r][3][:],
-                                    in1=sums[r, "kept"][:], op=ALU.add)
-            store(chunk, helped)
+        def helped_2(r, i):
+            chunk, blocks = place(r)
+            nc.vector.tensor_tensor(out=out_of(chunk, blocks[i]), in0=banks[r][2 + i][:],
+                                    in1=sums[r, "kept", i][:], op=ALU.add)
+            store(chunk, blocks[i])
 
         def plain_1(r):
-            chunk, plain, helped = place(r)
+            chunk, blocks = place(r)
             rest = mixing.tile([P, ROWS, P], F32)
             nc.vector.scalar_tensor_tensor(
-                out=rest[:], in0=banks[r][1][:], scalar=neg_sig_zeta[:, 0:1],
-                in1=state_of(chunk, plain), op0=ALU.mult, op1=ALU.add)
+                out=rest[:], in0=banks[r][0][:], scalar=neg_sig_zeta[:, 0:1],
+                in1=state_of(chunk, blocks[0]), op0=ALU.mult, op1=ALU.add)
             sums[r, "rest"] = rest
 
         def plain_2(r):
@@ -270,30 +306,41 @@ def tile_fastgrnncudacell_pa_kernel(
             sums[r, "gated"] = gated
 
         def plain_3(r):
-            chunk, plain, helped = place(r)
+            chunk, blocks = place(r)
             nc.vector.scalar_tensor_tensor(
-                out=out_of(chunk, plain), in0=banks[r][1][:], scalar=sig_sum[:, 0:1],
+                out=out_of(chunk, blocks[0]), in0=banks[r][0][:], scalar=sig_sum[:, 0:1],
                 in1=sums[r, "gated"][:], op0=ALU.mult, op1=ALU.add)
-            store(chunk, plain)
+            store(chunk, blocks[0])
 
         for r in range(AHEAD):
-            multiply_helped(r)
-            multiply_plain(r)
+            multiply(r, 1)
+            multiply(r, 0)
             activate(r)
         for r in range(N_ROUNDS):
             flip_first_half(r)
             if r + AHEAD < N_ROUNDS:
-                multiply_helped(r + AHEAD)
+                multiply(r + AHEAD, 1)
             flip_second_half(r)
             if r < PREPARE_STEPS:
                 prepare_step(1, r)
             if r + AHEAD < N_ROUNDS:
-                multiply_plain(r + AHEAD)
+                multiply(r + AHEAD, 0)
                 activate(r + AHEAD)
-            helped_1(r)
-            plain_1(r)
-            if r > 0:
+            helped_1(r, 1)
+            if both_helped(r):
+                helped_1(r, 0)
+            else:
+                plain_1(r)
+            if r > 0 and not both_helped(r - 1):
                 plain_3(r - 1)
-            plain_2(r)
-            helped_2(r)
-        plain_3(N_ROUNDS - 1)
+            if both_helped(r):
+                helped_2(r, 1)
+                helped_2(r, 0)
+            elif r > 0 and both_helped(r - 1):
+                helped_2(r, 1)
+                plain_2(r)
+            else:
+                plain_2(r)
+                helped_2(r, 1)
+        if not both_helped(N_ROUNDS - 1):
+            plain_3(N_ROUNDS - 1)

@@ -28,7 +28,7 @@ PREPARE_STEPS = PREPARE_BANKS + 1
 FLOPS = 2 * BATCH * HIDDEN * 2 * RANK
 
 
-BOTH_HELPED = (2, 5)
+BOTH_HELPED_LAST = 2
 
 
 def place(r):
@@ -37,7 +37,11 @@ def place(r):
 
 
 def both_helped(r):
-    return (r % ROUNDS_PER_CHUNK) in BOTH_HELPED
+    return r >= N_ROUNDS - BOTH_HELPED_LAST
+
+
+def plain_first(r):
+    return r > 0 and both_helped(r - 1) and not both_helped(r)
 
 
 def tile_fastgrnncudacell_pa_kernel(
@@ -259,13 +263,18 @@ def tile_fastgrnncudacell_pa_kernel(
                 first = gate_t[0]
             else:
                 first = cand_t[0]
-            second_bank = flip_back(gate_t[1], psum_once)
-            banks[r] = [flip_back(first, psum_twice), second_bank]
+            if plain_first(r):
+                first_bank = flip_back(first, psum_twice)
+                banks[r] = [first_bank, flip_back(gate_t[1], psum_once)]
+            else:
+                second_bank = flip_back(gate_t[1], psum_once)
+                banks[r] = [flip_back(first, psum_twice), second_bank]
 
         def flip_second_half(r):
             gate_t, cand_t, fresh_t = transposed[r]
             if both_helped(r):
-                banks[r].extend([flip_back(fresh_t[0], psum_once), flip_back(fresh_t[1], psum_once)])
+                last_bank = flip_back(fresh_t[1], psum_once)
+                banks[r].extend([flip_back(fresh_t[0], psum_once), last_bank])
             else:
                 banks[r].extend([flip_back(gate_t[0], psum_once), flip_back(fresh_t[1], psum_once)])
 
@@ -326,20 +335,23 @@ def tile_fastgrnncudacell_pa_kernel(
             if r + AHEAD < N_ROUNDS:
                 multiply(r + AHEAD, 0)
                 activate(r + AHEAD)
-            helped_1(r, 1)
-            if both_helped(r):
-                helped_1(r, 0)
-            else:
+            if plain_first(r):
                 plain_1(r)
-            if r > 0 and not both_helped(r - 1):
-                plain_3(r - 1)
-            if both_helped(r):
+                helped_1(r, 1)
+                plain_2(r)
+                helped_2(r, 1)
+            elif both_helped(r):
+                helped_1(r, 1)
+                helped_1(r, 0)
+                if r > 0 and not both_helped(r - 1):
+                    plain_3(r - 1)
                 helped_2(r, 1)
                 helped_2(r, 0)
-            elif r > 0 and both_helped(r - 1):
-                helped_2(r, 1)
-                plain_2(r)
             else:
+                helped_1(r, 1)
+                plain_1(r)
+                if r > 0:
+                    plain_3(r - 1)
                 plain_2(r)
                 helped_2(r, 1)
         if not both_helped(N_ROUNDS - 1):

@@ -84,7 +84,11 @@ def tile_fastgrnncudacell_pa_kernel(
         sig_nu = keep.tile([P, 1], F32)
         neg_sig_zeta = keep.tile([P, 1], F32)
         sig_sum = keep.tile([P, 1], F32)
+        idle_weights = keep.tile([P, P], BF16)
+        idle_columns = keep.tile([P, CHUNK], BF16)
 
+        nc.vector.memset(idle_weights[:], 0.0)
+        nc.vector.memset(idle_columns[:], 0.0)
         nc.vector.memset(w_scales[:].rearrange("p w n -> p (w n)").bitcast(I32), 0)
         nc.vector.memset(bias_rows[:], 0.0)
         make_identity(nc, ident[:])
@@ -160,20 +164,30 @@ def tile_fastgrnncudacell_pa_kernel(
                 in_=grouped[op][chunk][:, half * 8 * P : (half + 1) * 8 * P],
             )
 
+        idle_bank = psum_twice.tile([P, CHUNK], F32, tag="bank")
+
+        def keep_busy(count):
+            for i in range(count):
+                nc.tensor.matmul(out=idle_bank[:], lhsT=idle_weights[:], rhs=idle_columns[:],
+                                 start=True, stop=True)
+
         def prepare_step(chunk, step):
             if step < PREPARE_BANKS:
                 flip_and_copy(chunk, step)
             if step > 0:
                 quantise(chunk, step - 1)
 
+        keep_busy(4)
         for step in range(PREPARE_BANKS):
             prepare_step(0, step)
+            keep_busy(1)
 
         bias_flipped = psum_front.tile([P, P], F32, tag="front")
         nc.tensor.transpose(out=bias_flipped[:], in_=bias_rows_f32[:], identity=ident[:])
         nc.vector.tensor_copy(out=bias_cols[:], in_=bias_flipped[:, 0 : 2 * N_BLOCKS])
 
         prepare_step(0, PREPARE_BANKS)
+        keep_busy(2)
 
         nc.vector.tensor_scalar_mul(out=neg_sig_zeta[:], in0=sig_zeta[:], scalar1=-1.0)
         nc.vector.tensor_add(out=sig_sum[:], in0=sig_zeta[:], in1=sig_nu[:])

@@ -344,8 +344,8 @@ def tile_fastgrnncudacell_pa_kernel(
             if r + AHEAD < N_ROUNDS:
                 multiply(r + AHEAD, 1)
             flip_second_half(r)
-            if r < PREPARE_STEPS:
-                prepare_step(1, r)
+            if 1 <= r <= PREPARE_STEPS:
+                prepare_step(1, r - 1)
             if r + AHEAD < N_ROUNDS:
                 multiply(r + AHEAD, 0)
                 activate(r + AHEAD)

@@ -84,9 +84,12 @@ def tile_fastgrnncudacell_pa_kernel(
         sig_nu = keep.tile([P, 1], F32)
         neg_sig_zeta = keep.tile([P, 1], F32)
         sig_sum = keep.tile([P, 1], F32)
+        table_in = keep.tile([P, 1], F32)
+        table_out = keep.tile([P, 1], F32)
         idle_weights = keep.tile([P, P], BF16)
         idle_columns = keep.tile([P, CHUNK], BF16)
 
+        nc.vector.memset(table_in[:], 0.0)
         nc.vector.memset(idle_weights[:], 0.0)
         nc.vector.memset(idle_columns[:], 0.0)
         nc.vector.memset(w_scales[:].rearrange("p w n -> p (w n)").bitcast(I32), 0)
@@ -109,6 +112,11 @@ def tile_fastgrnncudacell_pa_kernel(
                 nc.sync.dma_start(out=w_words[:, op, cols].bitcast(I32), in_=words[0][:, cols].bitcast(I32))
 
         load_acts(0)
+        nc.sync.dma_start(out=bias_rows[0:N_BLOCKS, :], in_=bias_gate.rearrange("o (d j) -> (o d) j", j=P))
+        nc.sync.dma_start(out=bias_rows[N_BLOCKS : 2 * N_BLOCKS, :],
+                          in_=bias_update.rearrange("o (d j) -> (o d) j", j=P))
+        nc.sync.dma_start(out=zeta_sb[:], in_=zeta.rearrange("a b -> (a b)").partition_broadcast(P))
+        nc.sync.dma_start(out=nu_sb[:], in_=nu.rearrange("a b -> (a b)").partition_broadcast(P))
         for op, scales in enumerate((W2_scales, U2_scales)):
             for quad in range(4):
                 nc.sync.dma_start(
@@ -125,13 +133,7 @@ def tile_fastgrnncudacell_pa_kernel(
         for part in range(4):
             load_state(1, part)
 
-        nc.scalar.dma_start(out=zeta_sb[:], in_=zeta.rearrange("a b -> (a b)").partition_broadcast(P))
-        nc.scalar.dma_start(out=nu_sb[:], in_=nu.rearrange("a b -> (a b)").partition_broadcast(P))
-        nc.scalar.dma_start(out=bias_rows[0:N_BLOCKS, :],
-                            in_=bias_gate.rearrange("o (d j) -> (o d) j", j=P))
-        nc.scalar.dma_start(out=bias_rows[N_BLOCKS : 2 * N_BLOCKS, :],
-                            in_=bias_update.rearrange("o (d j) -> (o d) j", j=P))
-
+        nc.scalar.activation(out=table_out[:], in_=table_in[:], func=ACT.Sigmoid)
         nc.scalar.activation(out=sig_zeta[:], in_=zeta_sb[:], func=ACT.Sigmoid)
         nc.scalar.activation(out=sig_nu[:], in_=nu_sb[:], func=ACT.Sigmoid)
         nc.vector.tensor_copy(out=bias_rows_f32[:], in_=bias_rows[:])

@@ -29,6 +29,7 @@ FLOPS = 2 * BATCH * HIDDEN * 2 * RANK
 
 
 BOTH_HELPED_LAST = 2
+SCALAR_WEIGHTS_FROM = 8
 
 
 def place(r):
@@ -262,7 +263,7 @@ def tile_fastgrnncudacell_pa_kernel(
             else:
                 candidate_of(0)
                 gate_of(0)
-                weight_of(1, False)
+                weight_of(1, r >= SCALAR_WEIGHTS_FROM)
                 new_part_of(1)
             transposed[r] = (gates, cands, fresh)
 

from contextlib import ExitStack

import concourse.mybir as mybir
from concourse.masks import make_identity

F32 = mybir.dt.float32
BF16 = mybir.dt.bfloat16
I32 = mybir.dt.int32
U32 = mybir.dt.uint32
U8 = mybir.dt.uint8
FP8X4 = mybir.dt.float8_e4m3fn_x4
FP4X4 = mybir.dt.float4_e2m1fn_x4
ACT = mybir.ActivationFunctionType
ALU = mybir.AluOpType

P = 128
BATCH, RANK, HIDDEN = 1024, 512, 2048
CHUNK = 512
ROWS = CHUNK // P
N_CHUNKS = BATCH // CHUNK
N_BLOCKS = HIDDEN // P
ROUNDS_PER_CHUNK = N_BLOCKS // 2
N_ROUNDS = N_CHUNKS * ROUNDS_PER_CHUNK
AHEAD = 2
PREPARE_BANKS = 4
PREPARE_STEPS = PREPARE_BANKS + 1

FLOPS = 2 * BATCH * HIDDEN * 2 * RANK


BOTH_HELPED_LAST = 2
SCALAR_WEIGHTS_FROM = 8


def place(r):
    chunk, pair = divmod(r, ROUNDS_PER_CHUNK)
    return chunk, (2 * pair, 2 * pair + 1)


def both_helped(r):
    return r >= N_ROUNDS - BOTH_HELPED_LAST


def plain_first(r):
    return r > 0 and both_helped(r - 1) and not both_helped(r)


def tile_fastgrnncudacell_pa_kernel(
    tc, wx_r, uh_r, state, W2_words, W2_scales, U2_words, U2_scales,
    bias_gate, bias_update, zeta, nu, out,
):
    nc = tc.nc
    with ExitStack() as ctx:
        keep = ctx.enter_context(tc.tile_pool(name="keep", bufs=1))
        hidden_major = ctx.enter_context(tc.tile_pool(name="hidden_major", bufs=3 * 2))
        helped_pool = ctx.enter_context(tc.tile_pool(name="helped_pool", bufs=4))
        mixing = ctx.enter_context(tc.tile_pool(name="mixing", bufs=2))
        psum_front = ctx.enter_context(tc.psum_pool(name="psum_front", bufs=3))
        psum_twice = ctx.enter_context(tc.psum_pool(name="psum_twice", bufs=2))
        psum_once = ctx.enter_context(tc.psum_pool(name="psum_once", bufs=3))
        ctx.enter_context(tc.manual_schedule())

        acts_dram = [x.rearrange("(c p b) k -> c p (b k)", p=P, b=ROWS) for x in (wx_r, uh_r)]
        state_dram = state.rearrange("(c p b) n -> c p b n", p=P, b=ROWS)
        out_dram = out.rearrange("(c p b) n -> c p b n", p=P, b=ROWS)

        ident = keep.tile([P, P], F32)
        acts = [[keep.tile([P, ROWS * RANK], BF16, name="acts%d%d" % (op, chunk))
                 for chunk in range(N_CHUNKS)] for op in range(2)]
        grouped = [[keep.tile([P, 4 * CHUNK], BF16, name="grouped%d%d" % (op, chunk),
                              align_bytes=64)
                    for chunk in range(N_CHUNKS)] for op in range(2)]
        act_codes = keep.tile([P, 2, BATCH], U32, align_bytes=64)
        act_scales = keep.tile([P, 2, BATCH], U8, align_bytes=64)
        w_words = keep.tile([P, 2, 2 * HIDDEN], U8, align_bytes=64)
        w_scales = keep.tile([P, 2, HIDDEN], U8, align_bytes=64)
        state_sb = keep.tile([P, N_CHUNKS, ROWS, HIDDEN], BF16)
        out_sb = keep.tile([P, N_CHUNKS, ROWS, HIDDEN], F32)
        bias_rows = keep.tile([P, P], BF16)
        bias_rows_f32 = keep.tile([P, P], F32)
        bias_cols = keep.tile([P, 2 * N_BLOCKS], F32)
        zeta_sb = keep.tile([P, 1], BF16)
        nu_sb = keep.tile([P, 1], BF16)
        sig_zeta = keep.tile([P, 1], F32)
        sig_nu = keep.tile([P, 1], F32)
        neg_sig_zeta = keep.tile([P, 1], F32)
        sig_sum = keep.tile([P, 1], F32)
        table_in = keep.tile([P, 1], F32)
        table_out = keep.tile([P, 1], F32)
        idle_weights = keep.tile([P, P], BF16)
        idle_columns = keep.tile([P, CHUNK], BF16)

        nc.vector.memset(table_in[:], 0.0)
        nc.vector.memset(idle_weights[:], 0.0)
        nc.vector.memset(idle_columns[:], 0.0)
        nc.vector.memset(w_scales[:].rearrange("p w n -> p (w n)").bitcast(I32), 0)
        nc.vector.memset(bias_rows[:], 0.0)
        make_identity(nc, ident[:])

        def load_acts(chunk):
            for op in range(2):
                for half in range(2):
                    cols = slice(half * 2 * RANK, (half + 1) * 2 * RANK)
                    nc.sync.dma_start(out=acts[op][chunk][:, cols], in_=acts_dram[op][chunk][:, cols])

        def load_state(chunk, part):
            cols = slice(part * HIDDEN // 4, (part + 1) * HIDDEN // 4)
            nc.sync.dma_start(out=state_sb[:, chunk, :, cols], in_=state_dram[chunk][:, :, cols])

        def load_words(first_block, last_block):
            cols = slice(2 * first_block * P, 2 * last_block * P)
            for op, words in enumerate((W2_words, U2_words)):
                nc.sync.dma_start(out=w_words[:, op, cols].bitcast(I32), in_=words[0][:, cols].bitcast(I32))

        load_acts(0)
        nc.sync.dma_start(out=bias_rows[0:N_BLOCKS, :], in_=bias_gate.rearrange("o (d j) -> (o d) j", j=P))
        nc.sync.dma_start(out=bias_rows[N_BLOCKS : 2 * N_BLOCKS, :],
                          in_=bias_update.rearrange("o (d j) -> (o d) j", j=P))
        nc.sync.dma_start(out=zeta_sb[:], in_=zeta.rearrange("a b -> (a b)").partition_broadcast(P))
        nc.sync.dma_start(out=nu_sb[:], in_=nu.rearrange("a b -> (a b)").partition_broadcast(P))
        for op, scales in enumerate((W2_scales, U2_scales)):
            for quad in range(4):
                nc.sync.dma_start(
                    out=w_scales[32 * quad : 32 * quad + 4, op, :].bitcast(I32),
                    in_=scales[0, 4 * quad : 4 * quad + 4, :].bitcast(I32),
                )
        load_words(0, 4)
        load_state(0, 0)
        load_words(4, N_BLOCKS)
        load_state(0, 1)
        load_acts(1)
        load_state(0, 2)
        load_state(0, 3)
        for part in range(4):
            load_state(1, part)

        nc.scalar.activation(out=table_out[:], in_=table_in[:], func=ACT.Sigmoid)
        nc.scalar.activation(out=sig_zeta[:], in_=zeta_sb[:], func=ACT.Sigmoid)
        nc.scalar.activation(out=sig_nu[:], in_=nu_sb[:], func=ACT.Sigmoid)
        nc.vector.tensor_copy(out=bias_rows_f32[:], in_=bias_rows[:])

        def flip_and_copy(chunk, quarter):
            op, half = divmod(quarter, 2)
            words = acts[op][chunk][:].bitcast(F32).rearrange("p (b w) -> p b w", b=ROWS)
            halves = psum_front.tile([P, 2, 2 * P], F32, tag="front")
            for i in range(2):
                for u in range(2):
                    nc.tensor.transpose(
                        out=halves[:, u, i * P : (i + 1) * P],
                        in_=words[:, 2 * half + i, u : RANK // 2 : 2],
                        identity=ident[:],
                    )
            pairs = grouped[op][chunk][:].bitcast(F32).rearrange("p (n u) -> p n u", u=2)
            target = pairs[:, half * 2 * P : (half + 1) * 2 * P, :]
            source = halves[:].rearrange("p u n -> p n u")
            if chunk == 0 and half == 0:
                nc.vector.tensor_copy(out=target, in_=source)
            else:
                nc.scalar.copy(out=target, in_=source)

        def quantise(chunk, quarter):
            op, half = divmod(quarter, 2)
            first = chunk * CHUNK + half * 2 * P
            nc.vector.quantize_mx(
                out=act_codes[:, op, first : first + 2 * P].bitcast(FP8X4),
                scales=act_scales[:, op, first : first + 2 * P],
                in_=grouped[op][chunk][:, half * 8 * P : (half + 1) * 8 * P],
            )

        idle_bank = psum_twice.tile([P, CHUNK], F32, tag="bank")

        def keep_busy(count):
            for i in range(count):
                nc.tensor.matmul(out=idle_bank[:], lhsT=idle_weights[:], rhs=idle_columns[:],
                                 start=True, stop=True)

        def prepare_step(chunk, step):
            if step < PREPARE_BANKS:
                flip_and_copy(chunk, step)
            if step > 0:
                quantise(chunk, step - 1)

        keep_busy(4)
        for step in range(PREPARE_BANKS):
            prepare_step(0, step)
            keep_busy(1)

        bias_flipped = psum_front.tile([P, P], F32, tag="front")
        nc.tensor.transpose(out=bias_flipped[:], in_=bias_rows_f32[:], identity=ident[:])
        nc.vector.tensor_copy(out=bias_cols[:], in_=bias_flipped[:, 0 : 2 * N_BLOCKS])

        prepare_step(0, PREPARE_BANKS)
        keep_busy(2)

        nc.vector.tensor_scalar_mul(out=neg_sig_zeta[:], in0=sig_zeta[:], scalar1=-1.0)
        nc.vector.tensor_add(out=sig_sum[:], in0=sig_zeta[:], in1=sig_nu[:])

        products, transposed, banks, sums = {}, {}, {}, {}

        def multiply(r, i):
            chunk, blocks = place(r)
            d = blocks[i]
            cols = slice(chunk * CHUNK, (chunk + 1) * CHUNK)
            pre = psum_front.tile([P, CHUNK], F32, tag="front")
            for op in range(2):
                nc.tensor.matmul_mx(
                    out=pre[:],
                    lhsT=w_words[:, op, 2 * d * P : 2 * (d + 1) * P].bitcast(FP4X4),
                    lhsT_scale=w_scales[:, op, d * P : (d + 1) * P],
                    rhs=act_codes[:, op, cols].bitcast(FP8X4),
                    rhs_scale=act_scales[:, op, cols],
                    start=(op == 0),
                    stop=(op == 1),
                )
            products[r, i] = pre

        def activate(r):
            chunk, blocks = place(r)
            gates, cands, fresh = {}, {}, {}

            def gate_of(i):
                d = blocks[i]
                gate_t = hidden_major.tile([P, CHUNK], F32)
                nc.scalar.activation(out=gate_t[:], in_=products[r, i][:], func=ACT.Sigmoid,
                                     bias=bias_cols[:, d : d + 1])
                gates[i] = gate_t

            def candidate_of(i):
                d = blocks[i]
                cand_t = hidden_major.tile([P, CHUNK], F32)
                nc.scalar.activation(out=cand_t[:], in_=products[r, i][:], func=ACT.Tanh,
                                     bias=bias_cols[:, N_BLOCKS + d : N_BLOCKS + d + 1])
                cands[i] = cand_t

            weights = {}

            def weight_of(i, on_scalar):
                weight_t = helped_pool.tile([P, CHUNK], F32)
                if on_scalar:
                    nc.scalar.activation(out=weight_t[:], in_=gates[i][:], func=ACT.Identity,
                                         scale=neg_sig_zeta[:, 0:1], bias=sig_sum[:, 0:1])
                else:
                    nc.gpsimd.tensor_scalar(out=weight_t[:], in0=gates[i][:],
                                            scalar1=neg_sig_zeta[:, 0:1], scalar2=sig_sum[:, 0:1],
                                            op0=ALU.mult, op1=ALU.add)
                weights[i] = weight_t

            def new_part_of(i):
                weight_t = weights[i]
                fresh_t = helped_pool.tile([P, CHUNK], F32)
                nc.gpsimd.tensor_tensor(out=fresh_t[:], in0=weight_t[:], in1=cands[i][:], op=ALU.mult)
                fresh[i] = fresh_t

            gate_of(1)
            candidate_of(1)
            if both_helped(r):
                weight_of(1, True)
                new_part_of(1)
                gate_of(0)
                candidate_of(0)
                weight_of(0, True)
                new_part_of(0)
            else:
                candidate_of(0)
                gate_of(0)
                weight_of(1, r >= SCALAR_WEIGHTS_FROM)
                new_part_of(1)
            transposed[r] = (gates, cands, fresh)

        def flip_back(source, pool):
            bank = pool.tile([P, ROWS, P], F32)
            for b in range(ROWS):
                nc.tensor.transpose(out=bank[:, b, :], in_=source[:, b * P : (b + 1) * P],
                                    identity=ident[:])
            return bank

        def flip_first_half(r):
            gate_t, cand_t, fresh_t = transposed[r]
            if both_helped(r):
                first = gate_t[0]
            else:
                first = cand_t[0]
            if plain_first(r):
                first_bank = flip_back(first, psum_twice)
                banks[r] = [first_bank, flip_back(gate_t[1], psum_once)]
            else:
                second_bank = flip_back(gate_t[1], psum_once)
                banks[r] = [flip_back(first, psum_twice), second_bank]

        def flip_second_half(r):
            gate_t, cand_t, fresh_t = transposed[r]
            if both_helped(r):
                last_bank = flip_back(fresh_t[1], psum_once)
                banks[r].extend([flip_back(fresh_t[0], psum_once), last_bank])
            else:
                banks[r].extend([flip_back(gate_t[0], psum_once), flip_back(fresh_t[1], psum_once)])

        def state_of(chunk, d):
            return state_sb[:, chunk, :, d * P : (d + 1) * P]

        def out_of(chunk, d):
            return out_sb[:, chunk, :, d * P : (d + 1) * P]

        def store(chunk, d):
            nc.sync.dma_start(out=out_dram[chunk][:, :, d * P : (d + 1) * P], in_=out_of(chunk, d))

        def helped_1(r, i):
            chunk, blocks = place(r)
            kept = mixing.tile([P, ROWS, P], F32)
            nc.vector.tensor_tensor(out=kept[:], in0=banks[r][i][:], in1=state_of(chunk, blocks[i]),
                                    op=ALU.mult)
            sums[r, "kept", i] = kept

        def helped_2(r, i):
            chunk, blocks = place(r)
            nc.vector.tensor_tensor(out=out_of(chunk, blocks[i]), in0=banks[r][2 + i][:],
                                    in1=sums[r, "kept", i][:], op=ALU.add)
            store(chunk, blocks[i])

        def plain_1(r):
            chunk, blocks = place(r)
            rest = mixing.tile([P, ROWS, P], F32)
            nc.vector.scalar_tensor_tensor(
                out=rest[:], in0=banks[r][0][:], scalar=neg_sig_zeta[:, 0:1],
                in1=state_of(chunk, blocks[0]), op0=ALU.mult, op1=ALU.add)
            sums[r, "rest"] = rest

        def plain_2(r):
            gated = mixing.tile([P, ROWS, P], F32)
            nc.vector.tensor_tensor(out=gated[:], in0=sums[r, "rest"][:], in1=banks[r][2][:],
                                    op=ALU.mult)
            sums[r, "gated"] = gated

        def plain_3(r):
            chunk, blocks = place(r)
            nc.vector.scalar_tensor_tensor(
                out=out_of(chunk, blocks[0]), in0=banks[r][0][:], scalar=sig_sum[:, 0:1],
                in1=sums[r, "gated"][:], op0=ALU.mult, op1=ALU.add)
            store(chunk, blocks[0])

        for r in range(AHEAD):
            multiply(r, 1)
            multiply(r, 0)
            activate(r)
        for r in range(N_ROUNDS):
            flip_first_half(r)
            if r + AHEAD < N_ROUNDS:
                multiply(r + AHEAD, 1)
            flip_second_half(r)
            if 1 <= r <= PREPARE_STEPS:
                prepare_step(1, r - 1)
            if r + AHEAD < N_ROUNDS:
                multiply(r + AHEAD, 0)
                activate(r + AHEAD)
            if plain_first(r):
                plain_1(r)
                helped_1(r, 1)
                plain_2(r)
                helped_2(r, 1)
            elif both_helped(r):
                helped_1(r, 1)
                helped_1(r, 0)
                if r > 0 and not both_helped(r - 1):
                    plain_3(r - 1)
                helped_2(r, 1)
                helped_2(r, 0)
            else:
                helped_1(r, 1)
                plain_1(r)
                if r > 0:
                    plain_3(r - 1)
                plain_2(r)
                helped_2(r, 1)
        if not both_helped(N_ROUNDS - 1):
            plain_3(N_ROUNDS - 1)
